import numpy as np
import ml_dtypes


def mxq(x, axis, fmt="e4m3"):
    dtype, down = {"e4m3": (ml_dtypes.float8_e4m3fn, 7), "e5m2": (ml_dtypes.float8_e5m2, 14)}[fmt]
    v = np.moveaxis(np.asarray(x, np.float32).astype(ml_dtypes.bfloat16).astype(np.float64), axis, -1)
    blocks = v.reshape(v.shape[:-1] + (-1, 32))
    amax = np.abs(blocks).max(-1, keepdims=True)
    byte = np.maximum(np.where(amax > 0, np.frexp(amax)[1] - 1 + 127, 0) - down, 1)
    scale = np.exp2(byte - 127.0)
    codes = (blocks / scale).astype(np.float32).astype(dtype).astype(np.float64)
    return np.moveaxis((codes * scale).reshape(v.shape), -1, axis)


WIDE = False


def mx_kscale(k):
    if not WIDE:
        return np.ones(k)
    levels = np.array([10, -10, 5, -5, 0])
    a = np.random.permutation(np.resize(levels, k // 512 * 4)).reshape(k // 512, 4)
    idx = np.arange(k)
    return np.exp2(a[idx // 512, idx % 128 // 32])


BF16 = ml_dtypes.bfloat16


def bf(x):
    return np.asarray(x, np.float32).astype(BF16)


def f64(x):
    return np.asarray(x).astype(np.float64)


T, D, F, R = 8192, 128, 512, 128


def setup_inputs():
    s = mx_kscale(F)
    return {
        "h": bf(np.random.standard_normal((T, F)) * 0.75 * s),
        "ha": bf(np.random.standard_normal((T, R)) * 0.75),
        "W_down": bf(np.random.standard_normal((F, D)) / np.sqrt(F) / s[:, None]),
        "B_down": bf(np.random.standard_normal((R, D)) * 0.5 / np.sqrt(R)),
    }


def reference(h, ha, W_down, B_down):
    return (mxq(f64(h), 1, "e4m3") @ mxq(f64(W_down), 0, "e4m3")) + f64(ha) @ f64(B_down)

@@ -1,0 +1,198 @@
+from contextlib import ExitStack
+
+import concourse.mybir as mybir
+from concourse.masks import make_identity
+
+F32 = mybir.dt.float32
+BF16 = mybir.dt.bfloat16
+U32 = mybir.dt.uint32
+U8 = mybir.dt.uint8
+FP8X4 = mybir.dt.float8_e4m3fn_x4
+
+T, F, R, D = 8192, 512, 128, 128
+P = 128
+NT = T // P
+GT = 4
+NG = NT // GT
+FW = F // 2
+FLOPS = 2 * T * F * D + 2 * T * R * D
+
+H_CHUNKS = [4, 4, 8, 16, 16, 16]
+HA_CHUNKS = [8, 8, 16, 32]
+LOAD_ORDER = [("h", 0), ("a", 0), ("h", 1), ("h", 2), ("a", 1), ("h", 3), ("a", 2), ("h", 4), ("a", 3), ("h", 5)]
+ST = 8
+
+
+def tile_loramlp_pb_t_kernel(tc, h, ha, W_down, B_down, out):
+    nc = tc.nc
+    h2 = h.rearrange("(p t) k -> p (t k)", t=NT)
+    ha2 = ha.rearrange("(p t) r -> p (t r)", t=NT)
+    out2 = out.rearrange("(p t) d -> p (t d)", t=NT)
+
+    with ExitStack() as ctx:
+        const = ctx.enter_context(tc.tile_pool(name="const", bufs=1))
+        grp_pool = ctx.enter_context(tc.tile_pool(name="grp", bufs=4))
+        code_pool = ctx.enter_context(tc.tile_pool(name="code", bufs=3))
+        hat_pool = ctx.enter_context(tc.tile_pool(name="hat", bufs=3))
+        res_pool = ctx.enter_context(tc.tile_pool(name="res", bufs=NT // ST))
+        ps_xt = ctx.enter_context(tc.psum_pool(name="ps_xt", bufs=4))
+        ps_at = ctx.enter_context(tc.psum_pool(name="ps_at", bufs=1))
+        ps_pl = ctx.enter_context(tc.psum_pool(name="ps_pl", bufs=1))
+        ps_mx = ctx.enter_context(tc.psum_pool(name="ps_mx", bufs=2))
+        ctx.enter_context(tc.manual_schedule())
+
+        w_raw = const.tile([P, 4, D], BF16, name="w_raw")
+        nc.scalar.dma_start(
+            out=w_raw[:].rearrange("q (u e) d -> q u (e d)", u=2),
+            in_=W_down.rearrange("(u q e) d -> q u (e d)", u=2, e=2),
+        )
+        b_sb = const.tile([P, D], BF16, name="b_sb")
+        nc.scalar.dma_start(out=b_sb[:], in_=B_down)
+
+        h_word = {}
+        ha_tile = {}
+        h_start = [sum(H_CHUNKS[:c]) for c in range(len(H_CHUNKS))]
+        a_start = [sum(HA_CHUNKS[:c]) for c in range(len(HA_CHUNKS))]
+        for kind, c in LOAD_ORDER:
+            if kind == "h":
+                t0, n = h_start[c], H_CHUNKS[c]
+                h_sb = const.tile([P, n * F], BF16, name="h_sb%d" % c)
+                nc.sync.dma_start(out=h_sb[:], in_=h2[:, t0 * F : (t0 + n) * F])
+                words = h_sb[:].bitcast(F32)
+                for j in range(n):
+                    h_word[t0 + j] = words[:, j * FW : (j + 1) * FW]
+            else:
+                t0, n = a_start[c], HA_CHUNKS[c]
+                a_sb = const.tile([P, n * R], BF16, name="a_sb%d" % c)
+                nc.sync.dma_start(out=a_sb[:], in_=ha2[:, t0 * R : (t0 + n) * R])
+                for j in range(n):
+                    ha_tile[t0 + j] = a_sb[:, j * R : (j + 1) * R]
+
+        ident_f = const.tile([P, P], F32, name="ident_f")
+        make_identity(nc, ident_f[:])
+        ident_b = const.tile([P, P], BF16, name="ident_b")
+        make_identity(nc, ident_b[:])
+
+        w_grp = const.tile([P, D, 4], BF16, name="w_grp", align_bytes=64)
+        w_code = const.tile([P, D], U32, name="w_code", align_bytes=64)
+        w_scl = const.tile([P, D], U8, name="w_scl", align_bytes=64)
+
+        def prepare_w():
+            nc.vector.tensor_copy(out=w_grp[:], in_=w_raw[:].rearrange("q t d -> q d t"))
+            nc.vector.quantize_mx(
+                out=w_code[:].bitcast(FP8X4), scales=w_scl[:], in_=w_grp[:].rearrange("q d t -> q (d t)")
+            )
+
+        xt_of = {}
+        grp_of = {}
+        code_of = {}
+        scl_of = {}
+        at_of = {}
+        hat_of = {}
+        pl_of = {}
+        mx_of = {}
+        res_of = {}
+
+        def transpose_h(g):
+            for b in range(2):
+                xt = ps_xt.tile([P, 2 * 2 * P], F32, name="xt")
+                xt_of[(g, b)] = xt
+                for j in range(2):
+                    src = h_word[GT * g + 2 * b + j]
+                    for u in range(2):
+                        c0 = u * 2 * P + j * P
+                        nc.tensor.transpose(xt[:, c0 : c0 + P], src[:, u * P : (u + 1) * P], ident_f[:])
+
+        def transpose_ha(v):
+            at = ps_at.tile([P, 8 * P], BF16, name="at")
+            at_of[v] = at
+            for j in range(8):
+                nc.tensor.transpose(at[:, j * P : (j + 1) * P], ha_tile[8 * v + j], ident_b[:])
+
+        def copy_h(g, b, on_vector):
+            if b == 0:
+                grp = grp_pool.tile([P, GT * P * 4], BF16, name="grp", align_bytes=64)
+                grp_of[g] = grp
+            dst = grp_of[g][:].bitcast(F32)[:, b * 4 * P : (b + 1) * 4 * P].rearrange("q (n u) -> q n u", u=2)
+            src = xt_of[(g, b)][:].rearrange("q (u n) -> q n u", u=2)
+            if on_vector:
+                nc.vector.tensor_copy(out=dst, in_=src)
+            else:
+                nc.scalar.copy(out=dst, in_=src)
+
+        def copy_ha(v):
+            hat = hat_pool.tile([P, 8 * P], BF16, name="hat")
+            hat_of[v] = hat
+            nc.scalar.copy(out=hat[:], in_=at_of[v][:])
+
+        def quantise(g):
+            code = code_pool.tile([P, GT * P], U32, name="code", align_bytes=64)
+            scl = code_pool.tile([P, GT * P], U8, name="scl", align_bytes=64)
+            code_of[g] = code
+            scl_of[g] = scl
+            nc.vector.quantize_mx(out=code[:].bitcast(FP8X4), scales=scl[:], in_=grp_of[g][:])
+
+        def plain(g):
+            pl = ps_pl.tile([P, GT * D], F32, name="pl")
+            pl_of[g] = pl
+            hat = hat_of[g // 2]
+            for j in range(GT):
+                c0 = ((g % 2) * GT + j) * P
+                nc.tensor.matmul(
+                    pl[:, j * D : (j + 1) * D], lhsT=hat[:, c0 : c0 + P], rhs=b_sb[:], start=True, stop=True
+                )
+
+        def res_view(g):
+            s = (g * GT) // ST
+            if s not in res_of:
+                res = res_pool.tile([P, ST * D], F32, name="res")
+                res_of[s] = res
+            c0 = (g * GT - s * ST) * D
+            return res_of[s][:, c0 : c0 + GT * D]
+
+        def copy_plain(g):
+            nc.scalar.copy(out=res_view(g), in_=pl_of[g][:])
+
+        def mx(g):
+            acc = ps_mx.tile([P, GT * D], F32, name="acc")
+            mx_of[g] = acc
+            for j in range(GT):
+                nc.tensor.matmul_mx(
+                    out=acc[:, j * D : (j + 1) * D],
+                    lhsT=code_of[g][:, j * P : (j + 1) * P].bitcast(FP8X4),
+                    lhsT_scale=scl_of[g][:, j * P : (j + 1) * P],
+                    rhs=w_code[:].bitcast(FP8X4),
+                    rhs_scale=w_scl[:],
+                    start=True,
+                    stop=True,
+                )
+
+        def add_and_store(g):
+            nc.vector.tensor_tensor(out=res_view(g), in0=mx_of[g][:], in1=res_view(g), op=mybir.AluOpType.add)
+            t1 = (g + 1) * GT
+            if t1 % ST == 0:
+                s = t1 // ST - 1
+                nc.sync.dma_start(out=out2[:, s * ST * D : (s + 1) * ST * D], in_=res_of[s][:])
+
+        for i in range(-2, NG + 1):
+            if 0 <= i < NG:
+                quantise(i)
+            if i + 2 < NG:
+                transpose_h(i + 2)
+                if (i + 2) % 2 == 0:
+                    transpose_ha((i + 2) // 2)
+            if 0 <= i < NG:
+                copy_plain(i)
+            if 0 <= i + 1 < NG:
+                plain(i + 1)
+            if 0 <= i < NG:
+                mx(i)
+            if 0 <= i - 1 < NG:
+                add_and_store(i - 1)
+            if i == -1:
+                prepare_w()
+            if i + 2 < NG:
+                copy_h(i + 2, 0, False)
+                copy_h(i + 2, 1, (i + 2) % 2 == 0)
+                if (i + 2) % 2 == 0:
+                    copy_ha((i + 2) // 2)

@@ -17,9 +17,9 @@ NG = NT // GT
 FW = F // 2
 FLOPS = 2 * T * F * D + 2 * T * R * D
 
-H_CHUNKS = [4, 4, 8, 16, 16, 16]
-HA_CHUNKS = [8, 8, 16, 32]
-LOAD_ORDER = [("h", 0), ("a", 0), ("h", 1), ("h", 2), ("a", 1), ("h", 3), ("a", 2), ("h", 4), ("a", 3), ("h", 5)]
+H_CHUNKS = [4] * 16
+HA_CHUNKS = [8] * 8
+LOAD_ORDER = [x for v in range(8) for x in (("h", 2 * v), ("a", v), ("h", 2 * v + 1))]
 ST = 8
 
 

@@ -39,7 +39,6 @@ def tile_loramlp_pb_t_kernel(tc, h, ha, W_down, B_down, out):
         ps_at = ctx.enter_context(tc.psum_pool(name="ps_at", bufs=1))
         ps_pl = ctx.enter_context(tc.psum_pool(name="ps_pl", bufs=1))
         ps_mx = ctx.enter_context(tc.psum_pool(name="ps_mx", bufs=2))
-        ctx.enter_context(tc.manual_schedule())
 
         w_raw = const.tile([P, 4, D], BF16, name="w_raw")
         nc.scalar.dma_start(

@@ -20,7 +20,7 @@ FLOPS = 2 * T * F * D + 2 * T * R * D
 H_CHUNKS = [4] * 16
 HA_CHUNKS = [8] * 8
 LOAD_ORDER = [x for v in range(8) for x in (("h", 2 * v), ("a", v), ("h", 2 * v + 1))]
-ST = 8
+STORES = [8] * 7 + [4, 4]
 
 
 def tile_loramlp_pb_t_kernel(tc, h, ha, W_down, B_down, out):
@@ -34,11 +34,11 @@ def tile_loramlp_pb_t_kernel(tc, h, ha, W_down, B_down, out):
         grp_pool = ctx.enter_context(tc.tile_pool(name="grp", bufs=4))
         code_pool = ctx.enter_context(tc.tile_pool(name="code", bufs=3))
         hat_pool = ctx.enter_context(tc.tile_pool(name="hat", bufs=3))
-        res_pool = ctx.enter_context(tc.tile_pool(name="res", bufs=NT // ST))
+        res_pool = ctx.enter_context(tc.tile_pool(name="res", bufs=len(STORES)))
         ps_xt = ctx.enter_context(tc.psum_pool(name="ps_xt", bufs=4))
         ps_at = ctx.enter_context(tc.psum_pool(name="ps_at", bufs=1))
-        ps_pl = ctx.enter_context(tc.psum_pool(name="ps_pl", bufs=1))
-        ps_mx = ctx.enter_context(tc.psum_pool(name="ps_mx", bufs=2))
+        ps_pm = ctx.enter_context(tc.psum_pool(name="ps_pm", bufs=3))
+        ctx.enter_context(tc.manual_schedule())
 
         w_raw = const.tile([P, 4, D], BF16, name="w_raw")
         nc.scalar.dma_start(
@@ -131,29 +131,33 @@ def tile_loramlp_pb_t_kernel(tc, h, ha, W_down, B_down, out):
             scl_of[g] = scl
             nc.vector.quantize_mx(out=code[:].bitcast(FP8X4), scales=scl[:], in_=grp_of[g][:])
 
-        def plain(g):
-            pl = ps_pl.tile([P, GT * D], F32, name="pl")
-            pl_of[g] = pl
+        def plain(g, j0, j1):
+            if j0 == 0:
+                pl_new = ps_pm.tile([P, GT * D], F32, name="pm")
+                pl_of[g] = pl_new
+            pl = pl_of[g]
             hat = hat_of[g // 2]
-            for j in range(GT):
+            for j in range(j0, j1):
                 c0 = ((g % 2) * GT + j) * P
                 nc.tensor.matmul(
                     pl[:, j * D : (j + 1) * D], lhsT=hat[:, c0 : c0 + P], rhs=b_sb[:], start=True, stop=True
                 )
 
+        st_start = [sum(STORES[:s]) for s in range(len(STORES))]
+
         def res_view(g):
-            s = (g * GT) // ST
+            s = max(k for k in range(len(STORES)) if st_start[k] <= g * GT)
             if s not in res_of:
-                res = res_pool.tile([P, ST * D], F32, name="res")
+                res = res_pool.tile([P, max(STORES) * D], F32, name="res")
                 res_of[s] = res
-            c0 = (g * GT - s * ST) * D
+            c0 = (g * GT - st_start[s]) * D
             return res_of[s][:, c0 : c0 + GT * D]
 
         def copy_plain(g):
             nc.scalar.copy(out=res_view(g), in_=pl_of[g][:])
 
         def mx(g):
-            acc = ps_mx.tile([P, GT * D], F32, name="acc")
+            acc = ps_pm.tile([P, GT * D], F32, name="pm")
             mx_of[g] = acc
             for j in range(GT):
                 nc.tensor.matmul_mx(
@@ -169,9 +173,11 @@ def tile_loramlp_pb_t_kernel(tc, h, ha, W_down, B_down, out):
         def add_and_store(g):
             nc.vector.tensor_tensor(out=res_view(g), in0=mx_of[g][:], in1=res_view(g), op=mybir.AluOpType.add)
             t1 = (g + 1) * GT
-            if t1 % ST == 0:
-                s = t1 // ST - 1
-                nc.sync.dma_start(out=out2[:, s * ST * D : (s + 1) * ST * D], in_=res_of[s][:])
+            for s in range(len(STORES)):
+                if st_start[s] + STORES[s] == t1:
+                    nc.sync.dma_start(
+                        out=out2[:, st_start[s] * D : t1 * D], in_=res_of[s][:, : STORES[s] * D]
+                    )
 
         for i in range(-2, NG + 1):
             if 0 <= i < NG:
@@ -182,16 +188,19 @@ def tile_loramlp_pb_t_kernel(tc, h, ha, W_down, B_down, out):
                     transpose_ha((i + 2) // 2)
             if 0 <= i < NG:
                 copy_plain(i)
+            half = GT // 2 if i + 3 < NG else GT
             if 0 <= i + 1 < NG:
-                plain(i + 1)
+                plain(i + 1, 0, half)
             if 0 <= i < NG:
                 mx(i)
+            if 0 <= i + 1 < NG and half < GT:
+                plain(i + 1, half, GT)
             if 0 <= i - 1 < NG:
                 add_and_store(i - 1)
             if i == -1:
                 prepare_w()
             if i + 2 < NG:
                 copy_h(i + 2, 0, False)
-                copy_h(i + 2, 1, (i + 2) % 2 == 0)
+                copy_h(i + 2, 1, (i + 2) % 4 != 3 or i + 2 == NG - 1)
                 if (i + 2) % 2 == 0:
                     copy_ha((i + 2) // 2)

@@ -20,7 +20,7 @@ FLOPS = 2 * T * F * D + 2 * T * R * D
 H_CHUNKS = [4] * 16
 HA_CHUNKS = [8] * 8
 LOAD_ORDER = [x for v in range(8) for x in (("h", 2 * v), ("a", v), ("h", 2 * v + 1))]
-STORES = [8] * 7 + [4, 4]
+ST = 8
 
 
 def tile_loramlp_pb_t_kernel(tc, h, ha, W_down, B_down, out):
@@ -34,10 +34,11 @@ def tile_loramlp_pb_t_kernel(tc, h, ha, W_down, B_down, out):
         grp_pool = ctx.enter_context(tc.tile_pool(name="grp", bufs=4))
         code_pool = ctx.enter_context(tc.tile_pool(name="code", bufs=3))
         hat_pool = ctx.enter_context(tc.tile_pool(name="hat", bufs=3))
-        res_pool = ctx.enter_context(tc.tile_pool(name="res", bufs=len(STORES)))
+        res_pool = ctx.enter_context(tc.tile_pool(name="res", bufs=NT // ST))
         ps_xt = ctx.enter_context(tc.psum_pool(name="ps_xt", bufs=4))
         ps_at = ctx.enter_context(tc.psum_pool(name="ps_at", bufs=1))
-        ps_pm = ctx.enter_context(tc.psum_pool(name="ps_pm", bufs=3))
+        ps_pl = ctx.enter_context(tc.psum_pool(name="ps_pl", bufs=1))
+        ps_mx = ctx.enter_context(tc.psum_pool(name="ps_mx", bufs=2))
         ctx.enter_context(tc.manual_schedule())
 
         w_raw = const.tile([P, 4, D], BF16, name="w_raw")
@@ -131,33 +132,29 @@ def tile_loramlp_pb_t_kernel(tc, h, ha, W_down, B_down, out):
             scl_of[g] = scl
             nc.vector.quantize_mx(out=code[:].bitcast(FP8X4), scales=scl[:], in_=grp_of[g][:])
 
-        def plain(g, j0, j1):
-            if j0 == 0:
-                pl_new = ps_pm.tile([P, GT * D], F32, name="pm")
-                pl_of[g] = pl_new
-            pl = pl_of[g]
+        def plain(g):
+            pl = ps_pl.tile([P, GT * D], F32, name="pl")
+            pl_of[g] = pl
             hat = hat_of[g // 2]
-            for j in range(j0, j1):
+            for j in range(GT):
                 c0 = ((g % 2) * GT + j) * P
                 nc.tensor.matmul(
                     pl[:, j * D : (j + 1) * D], lhsT=hat[:, c0 : c0 + P], rhs=b_sb[:], start=True, stop=True
                 )
 
-        st_start = [sum(STORES[:s]) for s in range(len(STORES))]
-
         def res_view(g):
-            s = max(k for k in range(len(STORES)) if st_start[k] <= g * GT)
+            s = (g * GT) // ST
             if s not in res_of:
-                res = res_pool.tile([P, max(STORES) * D], F32, name="res")
+                res = res_pool.tile([P, ST * D], F32, name="res")
                 res_of[s] = res
-            c0 = (g * GT - st_start[s]) * D
+            c0 = (g * GT - s * ST) * D
             return res_of[s][:, c0 : c0 + GT * D]
 
         def copy_plain(g):
             nc.scalar.copy(out=res_view(g), in_=pl_of[g][:])
 
         def mx(g):
-            acc = ps_pm.tile([P, GT * D], F32, name="pm")
+            acc = ps_mx.tile([P, GT * D], F32, name="acc")
             mx_of[g] = acc
             for j in range(GT):
                 nc.tensor.matmul_mx(
@@ -173,11 +170,9 @@ def tile_loramlp_pb_t_kernel(tc, h, ha, W_down, B_down, out):
         def add_and_store(g):
             nc.vector.tensor_tensor(out=res_view(g), in0=mx_of[g][:], in1=res_view(g), op=mybir.AluOpType.add)
             t1 = (g + 1) * GT
-            for s in range(len(STORES)):
-                if st_start[s] + STORES[s] == t1:
-                    nc.sync.dma_start(
-                        out=out2[:, st_start[s] * D : t1 * D], in_=res_of[s][:, : STORES[s] * D]
-                    )
+            if t1 % ST == 0:
+                s = t1 // ST - 1
+                nc.sync.dma_start(out=out2[:, s * ST * D : (s + 1) * ST * D], in_=res_of[s][:])
 
         for i in range(-2, NG + 1):
             if 0 <= i < NG:
@@ -188,19 +183,16 @@ def tile_loramlp_pb_t_kernel(tc, h, ha, W_down, B_down, out):
                     transpose_ha((i + 2) // 2)
             if 0 <= i < NG:
                 copy_plain(i)
-            half = GT // 2 if i + 3 < NG else GT
             if 0 <= i + 1 < NG:
-                plain(i + 1, 0, half)
+                plain(i + 1)
             if 0 <= i < NG:
                 mx(i)
-            if 0 <= i + 1 < NG and half < GT:
-                plain(i + 1, half, GT)
             if 0 <= i - 1 < NG:
                 add_and_store(i - 1)
             if i == -1:
                 prepare_w()
             if i + 2 < NG:
                 copy_h(i + 2, 0, False)
-                copy_h(i + 2, 1, (i + 2) % 4 != 3 or i + 2 == NG - 1)
+                copy_h(i + 2, 1, (i + 2) % 2 == 0 or (i + 2) % 6 == 3)
                 if (i + 2) % 2 == 0:
                     copy_ha((i + 2) // 2)

from contextlib import ExitStack

import concourse.mybir as mybir
from concourse.masks import make_identity

F32 = mybir.dt.float32
BF16 = mybir.dt.bfloat16
U32 = mybir.dt.uint32
U8 = mybir.dt.uint8
FP8X4 = mybir.dt.float8_e4m3fn_x4

T, F, R, D = 8192, 512, 128, 128
P = 128
NT = T // P
GT = 4
NG = NT // GT
FW = F // 2
FLOPS = 2 * T * F * D + 2 * T * R * D

H_CHUNKS = [4] * 16
HA_CHUNKS = [8] * 8
LOAD_ORDER = [x for v in range(8) for x in (("h", 2 * v), ("a", v), ("h", 2 * v + 1))]
ST = 8


def tile_loramlp_pb_t_kernel(tc, h, ha, W_down, B_down, out):
    nc = tc.nc
    h2 = h.rearrange("(p t) k -> p (t k)", t=NT)
    ha2 = ha.rearrange("(p t) r -> p (t r)", t=NT)
    out2 = out.rearrange("(p t) d -> p (t d)", t=NT)

    with ExitStack() as ctx:
        const = ctx.enter_context(tc.tile_pool(name="const", bufs=1))
        grp_pool = ctx.enter_context(tc.tile_pool(name="grp", bufs=4))
        code_pool = ctx.enter_context(tc.tile_pool(name="code", bufs=3))
        hat_pool = ctx.enter_context(tc.tile_pool(name="hat", bufs=3))
        res_pool = ctx.enter_context(tc.tile_pool(name="res", bufs=NT // ST))
        ps_xt = ctx.enter_context(tc.psum_pool(name="ps_xt", bufs=4))
        ps_at = ctx.enter_context(tc.psum_pool(name="ps_at", bufs=1))
        ps_pl = ctx.enter_context(tc.psum_pool(name="ps_pl", bufs=1))
        ps_mx = ctx.enter_context(tc.psum_pool(name="ps_mx", bufs=2))
        ctx.enter_context(tc.manual_schedule())

        w_raw = const.tile([P, 4, D], BF16, name="w_raw")
        nc.scalar.dma_start(
            out=w_raw[:].rearrange("q (u e) d -> q u (e d)", u=2),
            in_=W_down.rearrange("(u q e) d -> q u (e d)", u=2, e=2),
        )
        b_sb = const.tile([P, D], BF16, name="b_sb")
        nc.scalar.dma_start(out=b_sb[:], in_=B_down)

        h_word = {}
        ha_tile = {}
        h_start = [sum(H_CHUNKS[:c]) for c in range(len(H_CHUNKS))]
        a_start = [sum(HA_CHUNKS[:c]) for c in range(len(HA_CHUNKS))]
        for kind, c in LOAD_ORDER:
            if kind == "h":
                t0, n = h_start[c], H_CHUNKS[c]
                h_sb = const.tile([P, n * F], BF16, name="h_sb%d" % c)
                nc.sync.dma_start(out=h_sb[:], in_=h2[:, t0 * F : (t0 + n) * F])
                words = h_sb[:].bitcast(F32)
                for j in range(n):
                    h_word[t0 + j] = words[:, j * FW : (j + 1) * FW]
            else:
                t0, n = a_start[c], HA_CHUNKS[c]
                a_sb = const.tile([P, n * R], BF16, name="a_sb%d" % c)
                nc.sync.dma_start(out=a_sb[:], in_=ha2[:, t0 * R : (t0 + n) * R])
                for j in range(n):
                    ha_tile[t0 + j] = a_sb[:, j * R : (j + 1) * R]

        ident_f = const.tile([P, P], F32, name="ident_f")
        make_identity(nc, ident_f[:])
        ident_b = const.tile([P, P], BF16, name="ident_b")
        make_identity(nc, ident_b[:])

        w_grp = const.tile([P, D, 4], BF16, name="w_grp", align_bytes=64)
        w_code = const.tile([P, D], U32, name="w_code", align_bytes=64)
        w_scl = const.tile([P, D], U8, name="w_scl", align_bytes=64)

        def prepare_w():
            nc.vector.tensor_copy(out=w_grp[:], in_=w_raw[:].rearrange("q t d -> q d t"))
            nc.vector.quantize_mx(
                out=w_code[:].bitcast(FP8X4), scales=w_scl[:], in_=w_grp[:].rearrange("q d t -> q (d t)")
            )

        xt_of = {}
        grp_of = {}
        code_of = {}
        scl_of = {}
        at_of = {}
        hat_of = {}
        pl_of = {}
        mx_of = {}
        res_of = {}

        def transpose_h(g):
            for b in range(2):
                xt = ps_xt.tile([P, 2 * 2 * P], F32, name="xt")
                xt_of[(g, b)] = xt
                for j in range(2):
                    src = h_word[GT * g + 2 * b + j]
                    for u in range(2):
                        c0 = u * 2 * P + j * P
                        nc.tensor.transpose(xt[:, c0 : c0 + P], src[:, u * P : (u + 1) * P], ident_f[:])

        def transpose_ha(v):
            at = ps_at.tile([P, 8 * P], BF16, name="at")
            at_of[v] = at
            for j in range(8):
                nc.tensor.transpose(at[:, j * P : (j + 1) * P], ha_tile[8 * v + j], ident_b[:])

        def copy_h(g, b, on_vector):
            if b == 0:
                grp = grp_pool.tile([P, GT * P * 4], BF16, name="grp", align_bytes=64)
                grp_of[g] = grp
            dst = grp_of[g][:].bitcast(F32)[:, b * 4 * P : (b + 1) * 4 * P].rearrange("q (n u) -> q n u", u=2)
            src = xt_of[(g, b)][:].rearrange("q (u n) -> q n u", u=2)
            if on_vector:
                nc.vector.tensor_copy(out=dst, in_=src)
            else:
                nc.scalar.copy(out=dst, in_=src)

        def copy_ha(v):
            hat = hat_pool.tile([P, 8 * P], BF16, name="hat")
            hat_of[v] = hat
            nc.scalar.copy(out=hat[:], in_=at_of[v][:])

        def quantise(g):
            code = code_pool.tile([P, GT * P], U32, name="code", align_bytes=64)
            scl = code_pool.tile([P, GT * P], U8, name="scl", align_bytes=64)
            code_of[g] = code
            scl_of[g] = scl
            nc.vector.quantize_mx(out=code[:].bitcast(FP8X4), scales=scl[:], in_=grp_of[g][:])

        def plain(g):
            pl = ps_pl.tile([P, GT * D], F32, name="pl")
            pl_of[g] = pl
            hat = hat_of[g // 2]
            for j in range(GT):
                c0 = ((g % 2) * GT + j) * P
                nc.tensor.matmul(
                    pl[:, j * D : (j + 1) * D], lhsT=hat[:, c0 : c0 + P], rhs=b_sb[:], start=True, stop=True
                )

        def res_view(g):
            s = (g * GT) // ST
            if s not in res_of:
                res = res_pool.tile([P, ST * D], F32, name="res")
                res_of[s] = res
            c0 = (g * GT - s * ST) * D
            return res_of[s][:, c0 : c0 + GT * D]

        def copy_plain(g):
            nc.scalar.copy(out=res_view(g), in_=pl_of[g][:])

        def mx(g):
            acc = ps_mx.tile([P, GT * D], F32, name="acc")
            mx_of[g] = acc
            for j in range(GT):
                nc.tensor.matmul_mx(
                    out=acc[:, j * D : (j + 1) * D],
                    lhsT=code_of[g][:, j * P : (j + 1) * P].bitcast(FP8X4),
                    lhsT_scale=scl_of[g][:, j * P : (j + 1) * P],
                    rhs=w_code[:].bitcast(FP8X4),
                    rhs_scale=w_scl[:],
                    start=True,
                    stop=True,
                )

        def add_and_store(g):
            nc.vector.tensor_tensor(out=res_view(g), in0=mx_of[g][:], in1=res_view(g), op=mybir.AluOpType.add)
            t1 = (g + 1) * GT
            if t1 % ST == 0:
                s = t1 // ST - 1
                nc.sync.dma_start(out=out2[:, s * ST * D : (s + 1) * ST * D], in_=res_of[s][:])

        for i in range(-2, NG + 1):
            if 0 <= i < NG:
                quantise(i)
            if i + 2 < NG:
                transpose_h(i + 2)
                if (i + 2) % 2 == 0:
                    transpose_ha((i + 2) // 2)
            if 0 <= i < NG:
                copy_plain(i)
            if 0 <= i + 1 < NG:
                plain(i + 1)
            if 0 <= i < NG:
                mx(i)
            if 0 <= i - 1 < NG:
                add_and_store(i - 1)
            if i == -1:
                prepare_w()
            if i + 2 < NG:
                copy_h(i + 2, 0, False)
                copy_h(i + 2, 1, (i + 2) % 2 == 0 or (i + 2) % 6 == 3)
                if (i + 2) % 2 == 0:
                    copy_ha((i + 2) // 2)
